import numpy as np
import ml_dtypes


def mxq(x, axis, fmt="e4m3"):
    dtype, down = {"e4m3": (ml_dtypes.float8_e4m3fn, 7), "e5m2": (ml_dtypes.float8_e5m2, 14)}[fmt]
    v = np.moveaxis(np.asarray(x, np.float32).astype(ml_dtypes.bfloat16).astype(np.float64), axis, -1)
    blocks = v.reshape(v.shape[:-1] + (-1, 32))
    amax = np.abs(blocks).max(-1, keepdims=True)
    byte = np.maximum(np.where(amax > 0, np.frexp(amax)[1] - 1 + 127, 0) - down, 1)
    scale = np.exp2(byte - 127.0)
    codes = (blocks / scale).astype(np.float32).astype(dtype).astype(np.float64)
    return np.moveaxis((codes * scale).reshape(v.shape), -1, axis)


WIDE = False


def mx_kscale(k):
    if not WIDE:
        return np.ones(k)
    levels = np.array([10, -10, 5, -5, 0])
    a = np.random.permutation(np.resize(levels, k // 512 * 4)).reshape(k // 512, 4)
    idx = np.arange(k)
    return np.exp2(a[idx // 512, idx % 128 // 32])


BF16 = ml_dtypes.bfloat16


def bf(x):
    return np.asarray(x, np.float32).astype(BF16)


def f64(x):
    return np.asarray(x).astype(np.float64)


S, B, D, H, F = 1024, 4, 512, 2, 2048
HD = D // H
EPS = 1e-8


def rmsnorm(x, w):
    ms = np.mean(x * x, axis=-1, keepdims=True)
    return w * (x / np.sqrt(ms + EPS))


def heads(t):
    return t.reshape(S, B, H, HD).transpose(1, 2, 0, 3)


def setup_inputs():
    s = mx_kscale(D)
    return {"x": bf(np.random.standard_normal((S, B, D))),
            "w_norm1": bf((1.0 + 0.1 * np.random.standard_normal(D)) * s),
            "in_proj_w": bf(np.random.standard_normal((3 * D, D)) / np.sqrt(D) / s[None, :]),
            "in_proj_b": bf(np.random.standard_normal(3 * D) * 0.3)}


def reference(x, w_norm1, in_proj_w, in_proj_b):
    h = rmsnorm(f64(x), f64(w_norm1))
    qkv = (mxq(h, 2, "e4m3") @ mxq(f64(in_proj_w), 1, "e4m3").T) + f64(in_proj_b)
    q, k, v = np.split(qkv, 3, axis=-1)
    return heads(q), heads(k), heads(v)

@@ -1,0 +1,165 @@
+from contextlib import ExitStack
+
+import concourse.mybir as mybir
+from concourse.masks import make_identity
+
+F32 = mybir.dt.float32
+BF16 = mybir.dt.bfloat16
+U32 = mybir.dt.uint32
+U8 = mybir.dt.uint8
+FP8X4 = mybir.dt.float8_e4m3fn_x4
+ACT = mybir.ActivationFunctionType
+ALU = mybir.AluOpType
+
+P = 128
+S, B, D = 1024, 4, 512
+HEADS, HD = 2, 256
+EPS = 1e-8
+PACK = 4
+ROWS = S // P
+CHUNK = 4
+PAIR = 2
+N_CHUNKS = B * ROWS // CHUNK
+W_TILES = D // P
+
+FLOPS = 2 * S * B * D * 3 * D
+
+
+def tile_transformerblock_pa_t_kernel(tc, x, w_norm1, in_proj_w, in_proj_b, out_0, out_1, out_2):
+    nc = tc.nc
+    outs = [out_0, out_1, out_2]
+    x_view = x.rearrange("(p j) b d -> p j b d", j=ROWS)
+    w_view = in_proj_w.rearrange("(c a p) d -> c p a d", c=3, a=W_TILES)
+
+    with ExitStack() as stack:
+        const = stack.enter_context(tc.tile_pool(name="const", bufs=1))
+        xin = stack.enter_context(tc.tile_pool(name="xin", bufs=N_CHUNKS))
+        wprep = stack.enter_context(tc.tile_pool(name="wprep", bufs=3))
+        stat = stack.enter_context(tc.tile_pool(name="stat", bufs=4))
+        work = stack.enter_context(tc.tile_pool(name="work", bufs=6))
+        result = stack.enter_context(tc.tile_pool(name="result", bufs=6))
+        psum_t = stack.enter_context(tc.psum_pool(name="psum_t", bufs=2))
+        psum_o = stack.enter_context(tc.psum_pool(name="psum_o", bufs=6))
+
+        gain = const.tile([P, D], BF16)
+        nc.scalar.dma_start(out=gain[:], in_=w_norm1.partition_broadcast(P))
+        bias = const.tile([P, 3 * D], BF16)
+        nc.scalar.dma_start(out=bias[:], in_=in_proj_b.partition_broadcast(P))
+
+        def load_x(n):
+            b, jq = divmod(n, ROWS // CHUNK)
+            xc = xin.tile([P, CHUNK, D], BF16, name="xc")
+            nc.sync.dma_start(out=xc[:], in_=x_view[:, jq * CHUNK : (jq + 1) * CHUNK, b, :])
+            return xc
+
+        x_chunks = [load_x(0)]
+        w_raws = []
+        for c in range(3):
+            w_raw = wprep.tile([P, W_TILES, D], BF16, name="w_raw")
+            nc.sync.dma_start(out=w_raw[:], in_=w_view[c])
+            w_raws.append(w_raw)
+        for n in range(1, N_CHUNKS):
+            x_chunks.append(load_x(n))
+
+        ident_bf = const.tile([P, P], BF16)
+        make_identity(nc, ident_bf[:])
+        ident_f32 = const.tile([P, P], F32)
+        make_identity(nc, ident_f32[:])
+        eps = const.tile([P, 1], F32)
+        nc.vector.memset(eps[:], EPS)
+        warm = const.tile([P, 1], F32)
+        nc.scalar.activation(out=warm[:], in_=eps[:], func=ACT.Sqrt)
+
+        w_codes, w_scales = [], []
+
+        def prepare_w(c):
+            w_grouped = wprep.tile([P, D * PACK], BF16, name="w_grouped", align_bytes=64)
+            words = w_grouped[:].bitcast(F32).rearrange("p (a r u) -> p a r u", a=W_TILES, u=2)
+            for half in range(W_TILES // PAIR):
+                wt = psum_t.tile([P, PAIR, 2, P], F32, name="wt", tag="t")
+                for i in range(PAIR):
+                    row_words = w_raws[c][:, half * PAIR + i, :].bitcast(F32)
+                    for u in range(2):
+                        nc.tensor.transpose(wt[:, i, u, :], row_words[:, u * P : (u + 1) * P], ident_f32[:])
+                nc.vector.tensor_copy(
+                    out=words[:, half * PAIR : (half + 1) * PAIR, :, :],
+                    in_=wt[:].rearrange("p a u r -> p a r u"),
+                )
+            codes = const.tile([P, D], U32, name="w_codes%d" % c, align_bytes=64)
+            scales = const.tile([P, D], U8, name="w_scales%d" % c, align_bytes=64)
+            nc.vector.quantize_mx(out=codes[:].bitcast(FP8X4), scales=scales[:], in_=w_grouped[:])
+            w_codes.append(codes)
+            w_scales.append(scales)
+
+        def front(n):
+            xc = x_chunks[n]
+            sumsq = stat.tile([P, CHUNK], F32, name="sumsq")
+            gained = []
+            for j in range(CHUNK):
+                y = work.tile([P, D], F32, name="y")
+                nc.gpsimd.tensor_tensor(out=y[:], in0=xc[:, j, :], in1=gain[:], op=ALU.mult)
+                gained.append(y)
+                squares = stat.tile([P, D], BF16, name="squares")
+                nc.scalar.activation(out=squares[:], in_=xc[:, j, :], func=ACT.Square, accum_out=sumsq[:, j : j + 1])
+            rms = stat.tile([P, CHUNK], F32, name="rms")
+            nc.scalar.activation(out=rms[:], in_=sumsq[:], func=ACT.Sqrt, scale=1.0 / D, bias=eps[:])
+            rstd = stat.tile([P, CHUNK], F32, name="rstd")
+            nc.vector.reciprocal(out=rstd[:], in_=rms[:])
+
+            operands = []
+            for pair in range(CHUNK // PAIR):
+                ht = psum_t.tile([P, PAIR, PACK, P], BF16, name="ht", tag="t")
+                for i in range(PAIR):
+                    j = pair * PAIR + i
+                    h = work.tile([P, D], BF16, name="h")
+                    nc.scalar.activation(out=h[:], in_=gained[j][:], func=ACT.Copy, scale=rstd[:, j : j + 1])
+                    h_cols = h[:].rearrange("p (u q e) -> p u e q", u=2, e=2)
+                    for t in range(PACK):
+                        nc.tensor.transpose(ht[:, i, t, :], h_cols[:, t // 2, t % 2, :], ident_bf[:])
+                grouped = work.tile([P, PAIR, P, PACK], BF16, name="grouped", align_bytes=64)
+                nc.scalar.copy(out=grouped[:], in_=ht[:].rearrange("p i t r -> p i r t"))
+                codes = work.tile([P, PAIR * P], U32, name="h_codes", align_bytes=64)
+                scales = work.tile([P, PAIR * P], U8, name="h_scales", align_bytes=64)
+                nc.vector.quantize_mx(
+                    out=codes[:].bitcast(FP8X4),
+                    scales=scales[:],
+                    in_=grouped[:].rearrange("p i r t -> p (i r t)"),
+                )
+                operands.append((codes, scales))
+            return operands
+
+        def back(n, operands):
+            b, jq = divmod(n, ROWS // CHUNK)
+            for c in range(3):
+                res = result.tile([P, HEADS, CHUNK, HD], F32, name="res")
+                bias_c = bias[:, c * D : (c + 1) * D].rearrange("p (h d) -> p h d", h=HEADS)
+                for j in range(CHUNK):
+                    codes, scales = operands[j // PAIR]
+                    cols = slice((j % PAIR) * P, (j % PAIR + 1) * P)
+                    acc = psum_o.tile([P, D], F32, name="acc")
+                    nc.tensor.matmul_mx(
+                        out=acc[:],
+                        lhsT=codes[:, cols].bitcast(FP8X4),
+                        lhsT_scale=scales[:, cols],
+                        rhs=w_codes[c][:].bitcast(FP8X4),
+                        rhs_scale=w_scales[c][:],
+                        start=True,
+                        stop=True,
+                    )
+                    nc.vector.tensor_tensor(
+                        out=res[:, :, j, :],
+                        in0=acc[:].rearrange("p (h d) -> p h d", h=HEADS),
+                        in1=bias_c,
+                        op=ALU.add,
+                    )
+                out_view = outs[c][b].rearrange("h (p j) d -> p h j d", j=ROWS)
+                nc.sync.dma_start(out=out_view[:, :, jq * CHUNK : (jq + 1) * CHUNK, :], in_=res[:])
+
+        prepare_w(0)
+        ready = front(0)
+        prepare_w(1)
+        prepare_w(2)
+        for n in range(N_CHUNKS):
+            following = front(n + 1) if n + 1 < N_CHUNKS else None
+            back(n, ready)
+            ready = following

@@ -41,10 +41,10 @@ def tile_transformerblock_pa_t_kernel(tc, x, w_norm1, in_proj_w, in_proj_b, out_
         psum_t = stack.enter_context(tc.psum_pool(name="psum_t", bufs=2))
         psum_o = stack.enter_context(tc.psum_pool(name="psum_o", bufs=6))
 
-        gain = const.tile([P, D], BF16)
-        nc.scalar.dma_start(out=gain[:], in_=w_norm1.partition_broadcast(P))
-        bias = const.tile([P, 3 * D], BF16)
-        nc.scalar.dma_start(out=bias[:], in_=in_proj_b.partition_broadcast(P))
+        vectors = const.tile([P, 4 * D], BF16)
+        nc.vector.memset(vectors[:], 0.0)
+        nc.scalar.dma_start(out=vectors[0:1, 0:D], in_=w_norm1.unsqueeze(0))
+        nc.scalar.dma_start(out=vectors[0:1, D : 4 * D], in_=in_proj_b.unsqueeze(0))
 
         def load_x(n):
             b, jq = divmod(n, ROWS // CHUNK)
@@ -69,6 +69,16 @@ def tile_transformerblock_pa_t_kernel(tc, x, w_norm1, in_proj_w, in_proj_b, out_
         nc.vector.memset(eps[:], EPS)
         warm = const.tile([P, 1], F32)
         nc.scalar.activation(out=warm[:], in_=eps[:], func=ACT.Sqrt)
+
+        ones = const.tile([P, P], BF16)
+        nc.vector.memset(ones[:], 1.0)
+        spread = const.tile([P, 4 * D], BF16)
+        for g in range(4):
+            copies = psum_o.tile([P, D], F32, name="copies", tag="acc")
+            nc.tensor.matmul(out=copies[:], lhsT=ones[:], rhs=vectors[:, g * D : (g + 1) * D], start=True, stop=True)
+            nc.vector.tensor_copy(out=spread[:, g * D : (g + 1) * D], in_=copies[:])
+        gain = spread[:, 0:D]
+        bias = spread[:, D : 4 * D]
 
         w_codes, w_scales = [], []
 
@@ -97,7 +107,7 @@ def tile_transformerblock_pa_t_kernel(tc, x, w_norm1, in_proj_w, in_proj_b, out_
             gained = []
             for j in range(CHUNK):
                 y = work.tile([P, D], F32, name="y")
-                nc.gpsimd.tensor_tensor(out=y[:], in0=xc[:, j, :], in1=gain[:], op=ALU.mult)
+                nc.gpsimd.tensor_tensor(out=y[:], in0=xc[:, j, :], in1=gain, op=ALU.mult)
                 gained.append(y)
                 squares = stat.tile([P, D], BF16, name="squares")
                 nc.scalar.activation(out=squares[:], in_=xc[:, j, :], func=ACT.Square, accum_out=sumsq[:, j : j + 1])
@@ -136,7 +146,7 @@ def tile_transformerblock_pa_t_kernel(tc, x, w_norm1, in_proj_w, in_proj_b, out_
                 for j in range(CHUNK):
                     codes, scales = operands[j // PAIR]
                     cols = slice((j % PAIR) * P, (j % PAIR + 1) * P)
-                    acc = psum_o.tile([P, D], F32, name="acc")
+                    acc = psum_o.tile([P, D], F32, name="acc", tag="acc")
                     nc.tensor.matmul_mx(
                         out=acc[:],
                         lhsT=codes[:, cols].bitcast(FP8X4),

@@ -116,7 +116,7 @@ def tile_transformerblock_pa_t_kernel(tc, x, w_norm1, in_proj_w, in_proj_b, out_
             rstd = stat.tile([P, CHUNK], F32, name="rstd")
             nc.vector.reciprocal(out=rstd[:], in_=rms[:])
 
-            operands = []
+            grouped = work.tile([P, CHUNK, P, PACK], BF16, name="grouped", align_bytes=64)
             for pair in range(CHUNK // PAIR):
                 ht = psum_t.tile([P, PAIR, PACK, P], BF16, name="ht", tag="t")
                 for i in range(PAIR):
@@ -126,26 +126,27 @@ def tile_transformerblock_pa_t_kernel(tc, x, w_norm1, in_proj_w, in_proj_b, out_
                     h_cols = h[:].rearrange("p (u q e) -> p u e q", u=2, e=2)
                     for t in range(PACK):
                         nc.tensor.transpose(ht[:, i, t, :], h_cols[:, t // 2, t % 2, :], ident_bf[:])
-                grouped = work.tile([P, PAIR, P, PACK], BF16, name="grouped", align_bytes=64)
-                nc.scalar.copy(out=grouped[:], in_=ht[:].rearrange("p i t r -> p i r t"))
-                codes = work.tile([P, PAIR * P], U32, name="h_codes", align_bytes=64)
-                scales = work.tile([P, PAIR * P], U8, name="h_scales", align_bytes=64)
-                nc.vector.quantize_mx(
-                    out=codes[:].bitcast(FP8X4),
-                    scales=scales[:],
-                    in_=grouped[:].rearrange("p i r t -> p (i r t)"),
+                nc.scalar.copy(
+                    out=grouped[:, pair * PAIR : (pair + 1) * PAIR, :, :],
+                    in_=ht[:].rearrange("p i t r -> p i r t"),
                 )
-                operands.append((codes, scales))
-            return operands
+            codes = work.tile([P, CHUNK * P], U32, name="h_codes", align_bytes=64)
+            scales = work.tile([P, CHUNK * P], U8, name="h_scales", align_bytes=64)
+            nc.vector.quantize_mx(
+                out=codes[:].bitcast(FP8X4),
+                scales=scales[:],
+                in_=grouped[:].rearrange("p j r t -> p (j r t)"),
+            )
+            return codes, scales
 
         def back(n, operands):
+            codes, scales = operands
             b, jq = divmod(n, ROWS // CHUNK)
             for c in range(3):
                 res = result.tile([P, HEADS, CHUNK, HD], F32, name="res")
                 bias_c = bias[:, c * D : (c + 1) * D].rearrange("p (h d) -> p h d", h=HEADS)
                 for j in range(CHUNK):
-                    codes, scales = operands[j // PAIR]
-                    cols = slice((j % PAIR) * P, (j % PAIR + 1) * P)
+                    cols = slice(j * P, (j + 1) * P)
                     acc = psum_o.tile([P, D], F32, name="acc", tag="acc")
                     nc.tensor.matmul_mx(
                         out=acc[:],

@@ -41,10 +41,11 @@ def tile_transformerblock_pa_t_kernel(tc, x, w_norm1, in_proj_w, in_proj_b, out_
         psum_t = stack.enter_context(tc.psum_pool(name="psum_t", bufs=2))
         psum_o = stack.enter_context(tc.psum_pool(name="psum_o", bufs=6))
 
-        vectors = const.tile([P, 4 * D], BF16)
-        nc.vector.memset(vectors[:], 0.0)
-        nc.scalar.dma_start(out=vectors[0:1, 0:D], in_=w_norm1.unsqueeze(0))
-        nc.scalar.dma_start(out=vectors[0:1, D : 4 * D], in_=in_proj_b.unsqueeze(0))
+        gain_row = const.tile([P, D], BF16)
+        nc.vector.memset(gain_row[:], 0.0)
+        nc.sync.dma_start(out=gain_row[0:1, :], in_=w_norm1.unsqueeze(0))
+        bias_row = const.tile([P, 3 * D], BF16)
+        nc.vector.memset(bias_row[:], 0.0)
 
         def load_x(n):
             b, jq = divmod(n, ROWS // CHUNK)
@@ -53,6 +54,7 @@ def tile_transformerblock_pa_t_kernel(tc, x, w_norm1, in_proj_w, in_proj_b, out_
             return xc
 
         x_chunks = [load_x(0)]
+        nc.sync.dma_start(out=bias_row[0:1, :], in_=in_proj_b.unsqueeze(0))
         w_raws = []
         for c in range(3):
             w_raw = wprep.tile([P, W_TILES, D], BF16, name="w_raw")
@@ -61,8 +63,6 @@ def tile_transformerblock_pa_t_kernel(tc, x, w_norm1, in_proj_w, in_proj_b, out_
         for n in range(1, N_CHUNKS):
             x_chunks.append(load_x(n))
 
-        ident_bf = const.tile([P, P], BF16)
-        make_identity(nc, ident_bf[:])
         ident_f32 = const.tile([P, P], F32)
         make_identity(nc, ident_f32[:])
         eps = const.tile([P, 1], F32)
@@ -72,13 +72,17 @@ def tile_transformerblock_pa_t_kernel(tc, x, w_norm1, in_proj_w, in_proj_b, out_
 
         ones = const.tile([P, P], BF16)
         nc.vector.memset(ones[:], 1.0)
-        spread = const.tile([P, 4 * D], BF16)
-        for g in range(4):
+
+        def spread(row, everywhere):
             copies = psum_o.tile([P, D], F32, name="copies", tag="acc")
-            nc.tensor.matmul(out=copies[:], lhsT=ones[:], rhs=vectors[:, g * D : (g + 1) * D], start=True, stop=True)
-            nc.vector.tensor_copy(out=spread[:, g * D : (g + 1) * D], in_=copies[:])
-        gain = spread[:, 0:D]
-        bias = spread[:, D : 4 * D]
+            nc.tensor.matmul(out=copies[:], lhsT=ones[:], rhs=row, start=True, stop=True)
+            nc.vector.tensor_copy(out=everywhere, in_=copies[:])
+
+        gain = const.tile([P, D], BF16)
+        spread(gain_row[:], gain[:])
+        bias = const.tile([P, 3 * D], BF16)
+        for c in range(3):
+            spread(bias_row[:, c * D : (c + 1) * D], bias[:, c * D : (c + 1) * D])
 
         w_codes, w_scales = [], []
 
@@ -107,7 +111,7 @@ def tile_transformerblock_pa_t_kernel(tc, x, w_norm1, in_proj_w, in_proj_b, out_
             gained = []
             for j in range(CHUNK):
                 y = work.tile([P, D], F32, name="y")
-                nc.gpsimd.tensor_tensor(out=y[:], in0=xc[:, j, :], in1=gain, op=ALU.mult)
+                nc.gpsimd.tensor_tensor(out=y[:], in0=xc[:, j, :], in1=gain[:], op=ALU.mult)
                 gained.append(y)
                 squares = stat.tile([P, D], BF16, name="squares")
                 nc.scalar.activation(out=squares[:], in_=xc[:, j, :], func=ACT.Square, accum_out=sumsq[:, j : j + 1])
@@ -116,37 +120,39 @@ def tile_transformerblock_pa_t_kernel(tc, x, w_norm1, in_proj_w, in_proj_b, out_
             rstd = stat.tile([P, CHUNK], F32, name="rstd")
             nc.vector.reciprocal(out=rstd[:], in_=rms[:])
 
-            grouped = work.tile([P, CHUNK, P, PACK], BF16, name="grouped", align_bytes=64)
+            operands = []
             for pair in range(CHUNK // PAIR):
-                ht = psum_t.tile([P, PAIR, PACK, P], BF16, name="ht", tag="t")
+                ht = psum_t.tile([P, PAIR, 2, P], F32, name="ht", tag="t")
                 for i in range(PAIR):
                     j = pair * PAIR + i
                     h = work.tile([P, D], BF16, name="h")
                     nc.scalar.activation(out=h[:], in_=gained[j][:], func=ACT.Copy, scale=rstd[:, j : j + 1])
-                    h_cols = h[:].rearrange("p (u q e) -> p u e q", u=2, e=2)
-                    for t in range(PACK):
-                        nc.tensor.transpose(ht[:, i, t, :], h_cols[:, t // 2, t % 2, :], ident_bf[:])
+                    h_words = h[:].bitcast(F32)
+                    for u in range(2):
+                        nc.tensor.transpose(ht[:, i, u, :], h_words[:, u * P : (u + 1) * P], ident_f32[:])
+                grouped = work.tile([P, PAIR * P * PACK], BF16, name="grouped", align_bytes=64)
                 nc.scalar.copy(
-                    out=grouped[:, pair * PAIR : (pair + 1) * PAIR, :, :],
-                    in_=ht[:].rearrange("p i t r -> p i r t"),
+                    out=grouped[:].bitcast(F32).rearrange("p (i r u) -> p i r u", i=PAIR, u=2),
+                    in_=ht[:].rearrange("p i u r -> p i r u"),
                 )
-            codes = work.tile([P, CHUNK * P], U32, name="h_codes", align_bytes=64)
-            scales = work.tile([P, CHUNK * P], U8, name="h_scales", align_bytes=64)
-            nc.vector.quantize_mx(
-                out=codes[:].bitcast(FP8X4),
-                scales=scales[:],
-                in_=grouped[:].rearrange("p j r t -> p (j r t)"),
-            )
-            return codes, scales
+                codes = work.tile([P, PAIR * P], U32, name="h_codes", align_bytes=64)
+                scales = work.tile([P, PAIR * P], U8, name="h_scales", align_bytes=64)
+                nc.vector.quantize_mx(
+                    out=codes[:].bitcast(FP8X4),
+                    scales=scales[:],
+                    in_=grouped[:],
+                )
+                operands.append((codes, scales))
+            return operands
 
         def back(n, operands):
-            codes, scales = operands
             b, jq = divmod(n, ROWS // CHUNK)
             for c in range(3):
                 res = result.tile([P, HEADS, CHUNK, HD], F32, name="res")
                 bias_c = bias[:, c * D : (c + 1) * D].rearrange("p (h d) -> p h d", h=HEADS)
                 for j in range(CHUNK):
-                    cols = slice(j * P, (j + 1) * P)
+                    codes, scales = operands[j // PAIR]
+                    cols = slice((j % PAIR) * P, (j % PAIR + 1) * P)
                     acc = psum_o.tile([P, D], F32, name="acc", tag="acc")
                     nc.tensor.matmul_mx(
                         out=acc[:],

from contextlib import ExitStack

import concourse.mybir as mybir
from concourse.masks import make_identity

F32 = mybir.dt.float32
BF16 = mybir.dt.bfloat16
U32 = mybir.dt.uint32
U8 = mybir.dt.uint8
FP8X4 = mybir.dt.float8_e4m3fn_x4
ACT = mybir.ActivationFunctionType
ALU = mybir.AluOpType

P = 128
S, B, D = 1024, 4, 512
HEADS, HD = 2, 256
EPS = 1e-8
PACK = 4
ROWS = S // P
CHUNK = 4
PAIR = 2
N_CHUNKS = B * ROWS // CHUNK
W_TILES = D // P

FLOPS = 2 * S * B * D * 3 * D


def tile_transformerblock_pa_t_kernel(tc, x, w_norm1, in_proj_w, in_proj_b, out_0, out_1, out_2):
    nc = tc.nc
    outs = [out_0, out_1, out_2]
    x_view = x.rearrange("(p j) b d -> p j b d", j=ROWS)
    w_view = in_proj_w.rearrange("(c a p) d -> c p a d", c=3, a=W_TILES)

    with ExitStack() as stack:
        const = stack.enter_context(tc.tile_pool(name="const", bufs=1))
        xin = stack.enter_context(tc.tile_pool(name="xin", bufs=N_CHUNKS))
        wprep = stack.enter_context(tc.tile_pool(name="wprep", bufs=3))
        stat = stack.enter_context(tc.tile_pool(name="stat", bufs=4))
        work = stack.enter_context(tc.tile_pool(name="work", bufs=6))
        result = stack.enter_context(tc.tile_pool(name="result", bufs=6))
        psum_t = stack.enter_context(tc.psum_pool(name="psum_t", bufs=2))
        psum_o = stack.enter_context(tc.psum_pool(name="psum_o", bufs=6))

        gain_row = const.tile([P, D], BF16)
        nc.vector.memset(gain_row[:], 0.0)
        nc.sync.dma_start(out=gain_row[0:1, :], in_=w_norm1.unsqueeze(0))
        bias_row = const.tile([P, 3 * D], BF16)
        nc.vector.memset(bias_row[:], 0.0)

        def load_x(n):
            b, jq = divmod(n, ROWS // CHUNK)
            xc = xin.tile([P, CHUNK, D], BF16, name="xc")
            nc.sync.dma_start(out=xc[:], in_=x_view[:, jq * CHUNK : (jq + 1) * CHUNK, b, :])
            return xc

        x_chunks = [load_x(0)]
        nc.sync.dma_start(out=bias_row[0:1, :], in_=in_proj_b.unsqueeze(0))
        w_raws = []
        for c in range(3):
            w_raw = wprep.tile([P, W_TILES, D], BF16, name="w_raw")
            nc.sync.dma_start(out=w_raw[:], in_=w_view[c])
            w_raws.append(w_raw)
        for n in range(1, N_CHUNKS):
            x_chunks.append(load_x(n))

        ident_f32 = const.tile([P, P], F32)
        make_identity(nc, ident_f32[:])
        eps = const.tile([P, 1], F32)
        nc.vector.memset(eps[:], EPS)
        warm = const.tile([P, 1], F32)
        nc.scalar.activation(out=warm[:], in_=eps[:], func=ACT.Sqrt)

        ones = const.tile([P, P], BF16)
        nc.vector.memset(ones[:], 1.0)

        def spread(row, everywhere):
            copies = psum_o.tile([P, D], F32, name="copies", tag="acc")
            nc.tensor.matmul(out=copies[:], lhsT=ones[:], rhs=row, start=True, stop=True)
            nc.vector.tensor_copy(out=everywhere, in_=copies[:])

        gain = const.tile([P, D], BF16)
        spread(gain_row[:], gain[:])
        bias = const.tile([P, 3 * D], BF16)
        for c in range(3):
            spread(bias_row[:, c * D : (c + 1) * D], bias[:, c * D : (c + 1) * D])

        w_codes, w_scales = [], []

        def prepare_w(c):
            w_grouped = wprep.tile([P, D * PACK], BF16, name="w_grouped", align_bytes=64)
            words = w_grouped[:].bitcast(F32).rearrange("p (a r u) -> p a r u", a=W_TILES, u=2)
            for half in range(W_TILES // PAIR):
                wt = psum_t.tile([P, PAIR, 2, P], F32, name="wt", tag="t")
                for i in range(PAIR):
                    row_words = w_raws[c][:, half * PAIR + i, :].bitcast(F32)
                    for u in range(2):
                        nc.tensor.transpose(wt[:, i, u, :], row_words[:, u * P : (u + 1) * P], ident_f32[:])
                nc.vector.tensor_copy(
                    out=words[:, half * PAIR : (half + 1) * PAIR, :, :],
                    in_=wt[:].rearrange("p a u r -> p a r u"),
                )
            codes = const.tile([P, D], U32, name="w_codes%d" % c, align_bytes=64)
            scales = const.tile([P, D], U8, name="w_scales%d" % c, align_bytes=64)
            nc.vector.quantize_mx(out=codes[:].bitcast(FP8X4), scales=scales[:], in_=w_grouped[:])
            w_codes.append(codes)
            w_scales.append(scales)

        def front(n):
            xc = x_chunks[n]
            sumsq = stat.tile([P, CHUNK], F32, name="sumsq")
            gained = []
            for j in range(CHUNK):
                y = work.tile([P, D], F32, name="y")
                nc.gpsimd.tensor_tensor(out=y[:], in0=xc[:, j, :], in1=gain[:], op=ALU.mult)
                gained.append(y)
                squares = stat.tile([P, D], BF16, name="squares")
                nc.scalar.activation(out=squares[:], in_=xc[:, j, :], func=ACT.Square, accum_out=sumsq[:, j : j + 1])
            rms = stat.tile([P, CHUNK], F32, name="rms")
            nc.scalar.activation(out=rms[:], in_=sumsq[:], func=ACT.Sqrt, scale=1.0 / D, bias=eps[:])
            rstd = stat.tile([P, CHUNK], F32, name="rstd")
            nc.vector.reciprocal(out=rstd[:], in_=rms[:])

            operands = []
            for pair in range(CHUNK // PAIR):
                ht = psum_t.tile([P, PAIR, 2, P], F32, name="ht", tag="t")
                for i in range(PAIR):
                    j = pair * PAIR + i
                    h = work.tile([P, D], BF16, name="h")
                    nc.scalar.activation(out=h[:], in_=gained[j][:], func=ACT.Copy, scale=rstd[:, j : j + 1])
                    h_words = h[:].bitcast(F32)
                    for u in range(2):
                        nc.tensor.transpose(ht[:, i, u, :], h_words[:, u * P : (u + 1) * P], ident_f32[:])
                grouped = work.tile([P, PAIR * P * PACK], BF16, name="grouped", align_bytes=64)
                nc.scalar.copy(
                    out=grouped[:].bitcast(F32).rearrange("p (i r u) -> p i r u", i=PAIR, u=2),
                    in_=ht[:].rearrange("p i u r -> p i r u"),
                )
                codes = work.tile([P, PAIR * P], U32, name="h_codes", align_bytes=64)
                scales = work.tile([P, PAIR * P], U8, name="h_scales", align_bytes=64)
                nc.vector.quantize_mx(
                    out=codes[:].bitcast(FP8X4),
                    scales=scales[:],
                    in_=grouped[:],
                )
                operands.append((codes, scales))
            return operands

        def back(n, operands):
            b, jq = divmod(n, ROWS // CHUNK)
            for c in range(3):
                res = result.tile([P, HEADS, CHUNK, HD], F32, name="res")
                bias_c = bias[:, c * D : (c + 1) * D].rearrange("p (h d) -> p h d", h=HEADS)
                for j in range(CHUNK):
                    codes, scales = operands[j // PAIR]
                    cols = slice((j % PAIR) * P, (j % PAIR + 1) * P)
                    acc = psum_o.tile([P, D], F32, name="acc", tag="acc")
                    nc.tensor.matmul_mx(
                        out=acc[:],
                        lhsT=codes[:, cols].bitcast(FP8X4),
                        lhsT_scale=scales[:, cols],
                        rhs=w_codes[c][:].bitcast(FP8X4),
                        rhs_scale=w_scales[c][:],
                        start=True,
                        stop=True,
                    )
                    nc.vector.tensor_tensor(
                        out=res[:, :, j, :],
                        in0=acc[:].rearrange("p (h d) -> p h d", h=HEADS),
                        in1=bias_c,
                        op=ALU.add,
                    )
                out_view = outs[c][b].rearrange("h (p j) d -> p h j d", j=ROWS)
                nc.sync.dma_start(out=out_view[:, :, jq * CHUNK : (jq + 1) * CHUNK, :], in_=res[:])

        prepare_w(0)
        ready = front(0)
        prepare_w(1)
        prepare_w(2)
        for n in range(N_CHUNKS):
            following = front(n + 1) if n + 1 < N_CHUNKS else None
            back(n, ready)
            ready = following
